import numpy as np
import ml_dtypes


def mxq(x, axis, fmt="e4m3"):
    dtype, down = {"e4m3": (ml_dtypes.float8_e4m3fn, 7), "e5m2": (ml_dtypes.float8_e5m2, 14)}[fmt]
    v = np.moveaxis(np.asarray(x, np.float32).astype(ml_dtypes.bfloat16).astype(np.float64), axis, -1)
    blocks = v.reshape(v.shape[:-1] + (-1, 32))
    amax = np.abs(blocks).max(-1, keepdims=True)
    byte = np.maximum(np.where(amax > 0, np.frexp(amax)[1] - 1 + 127, 0) - down, 1)
    scale = np.exp2(byte - 127.0)
    codes = (blocks / scale).astype(np.float32).astype(dtype).astype(np.float64)
    return np.moveaxis((codes * scale).reshape(v.shape), -1, axis)


WIDE = False


def mx_kscale(k):
    if not WIDE:
        return np.ones(k)
    levels = np.array([10, -10, 5, -5, 0])
    a = np.random.permutation(np.resize(levels, k // 512 * 4)).reshape(k // 512, 4)
    idx = np.arange(k)
    return np.exp2(a[idx // 512, idx % 128 // 32])


BF16 = ml_dtypes.bfloat16


def bf(x):
    return np.asarray(x, np.float32).astype(BF16)


def f64(x):
    return np.asarray(x).astype(np.float64)


E2M1 = np.array([0.0, 0.5, 1.0, 1.5, 2.0, 3.0, 4.0, 6.0, -0.0, -0.5, -1.0, -1.5, -2.0, -3.0, -4.0, -6.0])


def pack_weight(w, fmt):
    k, n = w.shape
    w = f64(bf(w)).reshape(k // 32, 32, n)
    amax = np.abs(w).max(1)
    if fmt == "e4m3":
        byte = np.frexp(amax)[1] - 1 + 127 - 7
    else:
        mant, ex = np.frexp(amax / 6.0)
        byte = np.where(mant > 0.5, ex, ex - 1) + 127
    byte = np.clip(np.where(amax > 0, byte, 1), 1, 254)
    scaled = (w * np.exp2(127.0 - byte)[:, None, :]).reshape(k, n).astype(np.float32)
    by_word = np.ascontiguousarray(scaled.reshape(k // 512, 128, 4, n).transpose(0, 1, 3, 2))
    if fmt == "e4m3":
        words = by_word.astype(ml_dtypes.float8_e4m3fn).view(np.uint8)
    else:
        c = by_word.astype(ml_dtypes.float4_e2m1fn).view(np.uint8) & 0xF
        words = c[..., 0::2] | (c[..., 1::2] << 4)
    return np.ascontiguousarray(words), np.ascontiguousarray(byte.astype(np.uint8).reshape(k // 512, 16, n))


def unpack_weight(words, scales, fmt):
    g, p, n, _ = words.shape
    if fmt == "e4m3":
        vals = np.ascontiguousarray(words).view(ml_dtypes.float8_e4m3fn).astype(np.float64)
    else:
        nib = np.empty((g, p, n, 4), np.uint8)
        nib[..., 0::2] = words & 0xF
        nib[..., 1::2] = words >> 4
        vals = E2M1[nib]
    vals = vals * np.repeat(np.exp2(scales.astype(np.float64) - 127.0), 8, axis=1)[..., None]
    return vals.transpose(0, 1, 3, 2).reshape(g * 512, n)


B, N, D, R, Q = 4, 4096, 512, 8, 16


def setup_inputs():
    s = mx_kscale(D)
    x = bf(np.random.standard_normal((B, N, D)) * s)
    w0 = bf(np.random.standard_normal((B, N, R)))
    core1 = np.random.standard_normal((R, D, Q)) / np.sqrt(D * R) / s[None, :, None]
    core2 = np.random.standard_normal((Q, D, R)) / np.sqrt(D * Q) / s[None, :, None]
    core1_words, core1_scales = pack_weight(core1.reshape(-1, Q), "e4m3")
    core2_words, core2_scales = pack_weight(core2.reshape(-1, R), "e4m3")
    return {"x": x,
            "w0": w0,
            "core1_words": core1_words, "core1_scales": core1_scales,
            "core2_words": core2_words, "core2_scales": core2_scales}


def reference(x, w0, core1_words, core1_scales, core2_words, core2_scales):
    xq = mxq(f64(x), 2, "e4m3")
    c1 = unpack_weight(core1_words, core1_scales, "e4m3").reshape(R, D, Q).transpose(1, 0, 2).reshape(D, R * Q)
    c2 = unpack_weight(core2_words, core2_scales, "e4m3").reshape(Q, D, R).transpose(1, 0, 2).reshape(D, Q * R)
    m1 = (xq @ c1).reshape(B, N, R, Q)
    m2 = (xq @ c2).reshape(B, N, Q, R)
    w1 = (f64(w0)[..., :, None] * m1).sum(-2)
    w2 = (w1[..., :, None] * m2).sum(-2)
    return w2

@@ -1,0 +1,156 @@
+from contextlib import ExitStack
+
+import concourse.mybir as mybir
+from concourse.masks import make_identity
+
+F32 = mybir.dt.float32
+BF16 = mybir.dt.bfloat16
+I32 = mybir.dt.int32
+U32 = mybir.dt.uint32
+U8 = mybir.dt.uint8
+FP8X4 = mybir.dt.float8_e4m3fn_x4
+MULT = mybir.AluOpType.mult
+ADD = mybir.AluOpType.add
+AXIS_X = mybir.AxisListType.X
+
+P = 128
+D = 512
+R = 8
+Q = 16
+RQ = R * Q
+TOKENS = 4 * 4096
+SLOTS = TOKENS // P
+GROUP = 4
+ROUNDS = SLOTS // GROUP
+HALF = 2
+STORE_ROUNDS = 4
+
+FLOPS = 2 * TOKENS * D * 2 * RQ + 2 * TOKENS * 2 * RQ
+
+
+def tile_linear_pa_t_e_kernel(
+    tc, x, w0, core1_words, core1_scales, core2_words, core2_scales, out
+):
+    nc = tc.nc
+    x_view = x.flatten_outer_dims().rearrange("(p j) d -> p j d", j=SLOTS)
+    w0_view = w0.flatten_outer_dims().rearrange("(p j) r -> p j r", j=SLOTS)
+    out_view = out.flatten_outer_dims().rearrange("(p j) r -> p j r", j=SLOTS)
+
+    with ExitStack() as stack:
+        keep = stack.enter_context(tc.tile_pool(name="keep", bufs=1))
+        x_pool = stack.enter_context(tc.tile_pool(name="x_pool", bufs=ROUNDS))
+        work = stack.enter_context(tc.tile_pool(name="work", bufs=3))
+        xt_pool = stack.enter_context(tc.psum_pool(name="xt_pool", bufs=4))
+        m_pool = stack.enter_context(tc.psum_pool(name="m_pool", bufs=2))
+
+        core_scales = keep.tile([P, 2 * RQ], U8, align_bytes=64)
+        nc.vector.memset(core_scales[:].bitcast(I32), 0)
+        identity = keep.tile([P, P], F32)
+        make_identity(nc, identity[:])
+
+        x_tiles = []
+
+        def load_x(i):
+            x_tile = x_pool.tile([P, GROUP, D], BF16, name="x_tile")
+            nc.sync.dma_start(out=x_tile[:], in_=x_view[:, i * GROUP : (i + 1) * GROUP, :])
+            x_tiles.append(x_tile)
+
+        load_x(0)
+
+        core_codes = keep.tile([P, 2 * RQ], U32, align_bytes=64)
+        nc.sync.dma_start(
+            out=core_codes[:, 0:RQ].bitcast(I32).rearrange("p (g n) -> p g n", g=R),
+            in_=core1_words.rearrange("g p n t -> p g (n t)").bitcast(I32),
+        )
+        nc.sync.dma_start(
+            out=core_codes[:, RQ : 2 * RQ].bitcast(I32).rearrange("p (g n) -> p g n", g=Q),
+            in_=core2_words.rearrange("g p n t -> p g (n t)").bitcast(I32),
+        )
+        for quadrant in range(4):
+            rows = slice(32 * quadrant, 32 * quadrant + 4)
+            blocks = slice(4 * quadrant, 4 * quadrant + 4)
+            nc.sync.dma_start(
+                out=core_scales[rows, 0:RQ].bitcast(I32).rearrange("j (g n) -> j g n", g=R),
+                in_=core1_scales[:, blocks, :].rearrange("g j n -> j g n").bitcast(I32),
+            )
+            nc.sync.dma_start(
+                out=core_scales[rows, RQ : 2 * RQ].bitcast(I32).rearrange("j (g n) -> j g n", g=Q),
+                in_=core2_scales[:, blocks, :].rearrange("g j n -> j g n").bitcast(I32),
+            )
+        w0_sb = keep.tile([P, SLOTS, R], BF16)
+        nc.sync.dma_start(out=w0_sb[:], in_=w0_view)
+
+        for i in range(1, ROUNDS):
+            load_x(i)
+
+        out_tile = None
+        for i in range(ROUNDS):
+            x_words = x_tiles[i][:].bitcast(F32)
+            grouped = work.tile([P, GROUP, P, 4], BF16, align_bytes=64)
+            grouped_words = grouped[:].bitcast(F32)
+            for h in range(GROUP // HALF):
+                xt = xt_pool.tile([P, HALF, 2, P], F32)
+                for a in range(HALF):
+                    for u in range(2):
+                        nc.tensor.transpose(
+                            xt[:, a, u, :], x_words[:, h * HALF + a, u : D // 2 : 2], identity[:]
+                        )
+                nc.scalar.copy(
+                    out=grouped_words[:, h * HALF : (h + 1) * HALF, :, :],
+                    in_=xt[:].rearrange("p a u r -> p a r u"),
+                )
+            x_codes = work.tile([P, GROUP * P], U32, align_bytes=64)
+            x_scales = work.tile([P, GROUP * P], U8, align_bytes=64)
+            nc.vector.quantize_mx(
+                out=x_codes[:].bitcast(FP8X4),
+                scales=x_scales[:],
+                in_=grouped[:].rearrange("p a r t -> p (a r t)"),
+            )
+
+            m1 = m_pool.tile([P, GROUP, RQ], F32)
+            m2 = m_pool.tile([P, GROUP, RQ], F32)
+            for c, m in enumerate((m1, m2)):
+                for a in range(GROUP):
+                    nc.tensor.matmul_mx(
+                        out=m[:, a, :],
+                        lhsT=x_codes[:, a * P : (a + 1) * P].bitcast(FP8X4),
+                        lhsT_scale=x_scales[:, a * P : (a + 1) * P],
+                        rhs=core_codes[:, c * RQ : (c + 1) * RQ].bitcast(FP8X4),
+                        rhs_scale=core_scales[:, c * RQ : (c + 1) * RQ],
+                        start=True,
+                        stop=True,
+                    )
+
+            slots = slice(i * GROUP, (i + 1) * GROUP)
+            p1 = work.tile([P, GROUP, R, Q], F32)
+            nc.vector.tensor_tensor(
+                out=p1[:],
+                in0=m1[:].rearrange("p a (r q) -> p a r q", r=R),
+                in1=w0_sb[:, slots, :].unsqueeze(3).to_broadcast([P, GROUP, R, Q]),
+                op=MULT,
+            )
+            w1 = work.tile([P, GROUP, Q], F32)
+            nc.vector.tensor_reduce(
+                out=w1[:], in_=p1[:].rearrange("p a r q -> p a q r"), axis=AXIS_X, op=ADD
+            )
+            p2 = work.tile([P, GROUP, Q, R], F32)
+            nc.vector.tensor_tensor(
+                out=p2[:],
+                in0=m2[:].rearrange("p a (q r) -> p a q r", q=Q),
+                in1=w1[:].unsqueeze(3).to_broadcast([P, GROUP, Q, R]),
+                op=MULT,
+            )
+            part = i % STORE_ROUNDS
+            if part == 0:
+                out_tile = work.tile([P, STORE_ROUNDS * GROUP, R], F32, name="out_tile")
+            nc.vector.tensor_reduce(
+                out=out_tile[:, part * GROUP : (part + 1) * GROUP, :],
+                in_=p2[:].rearrange("p a q r -> p a r q"),
+                axis=AXIS_X,
+                op=ADD,
+            )
+            if part == STORE_ROUNDS - 1:
+                first = (i + 1 - STORE_ROUNDS) * GROUP
+                nc.sync.dma_start(
+                    out=out_view[:, first : first + STORE_ROUNDS * GROUP, :], in_=out_tile[:]
+                )

@@ -122,22 +122,20 @@ def tile_linear_pa_t_e_kernel(
                     )
 
             slots = slice(i * GROUP, (i + 1) * GROUP)
-            p1 = work.tile([P, GROUP, R, Q], F32)
+            p1 = work.tile([P, GROUP, Q, R], F32)
             nc.vector.tensor_tensor(
                 out=p1[:],
-                in0=m1[:].rearrange("p a (r q) -> p a r q", r=R),
-                in1=w0_sb[:, slots, :].unsqueeze(3).to_broadcast([P, GROUP, R, Q]),
+                in0=m1[:].rearrange("p a (r q) -> p a q r", r=R),
+                in1=w0_sb[:, slots, :].unsqueeze(2).to_broadcast([P, GROUP, Q, R]),
                 op=MULT,
             )
             w1 = work.tile([P, GROUP, Q], F32)
-            nc.vector.tensor_reduce(
-                out=w1[:], in_=p1[:].rearrange("p a r q -> p a q r"), axis=AXIS_X, op=ADD
-            )
-            p2 = work.tile([P, GROUP, Q, R], F32)
+            nc.vector.tensor_reduce(out=w1[:], in_=p1[:], axis=AXIS_X, op=ADD)
+            p2 = work.tile([P, GROUP, R, Q], F32)
             nc.vector.tensor_tensor(
                 out=p2[:],
-                in0=m2[:].rearrange("p a (q r) -> p a q r", q=Q),
-                in1=w1[:].unsqueeze(3).to_broadcast([P, GROUP, Q, R]),
+                in0=m2[:].rearrange("p a (q r) -> p a r q", q=Q),
+                in1=w1[:].unsqueeze(2).to_broadcast([P, GROUP, R, Q]),
                 op=MULT,
             )
             part = i % STORE_ROUNDS
@@ -145,7 +143,7 @@ def tile_linear_pa_t_e_kernel(
                 out_tile = work.tile([P, STORE_ROUNDS * GROUP, R], F32, name="out_tile")
             nc.vector.tensor_reduce(
                 out=out_tile[:, part * GROUP : (part + 1) * GROUP, :],
-                in_=p2[:].rearrange("p a q r -> p a r q"),
+                in_=p2[:],
                 axis=AXIS_X,
                 op=ADD,
             )

@@ -39,9 +39,11 @@ def tile_linear_pa_t_e_kernel(
     with ExitStack() as stack:
         keep = stack.enter_context(tc.tile_pool(name="keep", bufs=1))
         x_pool = stack.enter_context(tc.tile_pool(name="x_pool", bufs=ROUNDS))
+        out_pool = stack.enter_context(tc.tile_pool(name="out_pool", bufs=ROUNDS // STORE_ROUNDS))
         work = stack.enter_context(tc.tile_pool(name="work", bufs=3))
         xt_pool = stack.enter_context(tc.psum_pool(name="xt_pool", bufs=4))
         m_pool = stack.enter_context(tc.psum_pool(name="m_pool", bufs=2))
+        stack.enter_context(tc.manual_schedule())
 
         core_scales = keep.tile([P, 2 * RQ], U8, align_bytes=64)
         nc.vector.memset(core_scales[:].bitcast(I32), 0)
@@ -83,13 +85,20 @@ def tile_linear_pa_t_e_kernel(
         for i in range(1, ROUNDS):
             load_x(i)
 
-        out_tile = None
-        for i in range(ROUNDS):
+        grouped_of = {}
+        codes_of = {}
+        m_of = {}
+        p1_of = {}
+        w1_of = {}
+        p2_of = {}
+        out_of = {}
+
+        def transpose(i):
             x_words = x_tiles[i][:].bitcast(F32)
-            grouped = work.tile([P, GROUP, P, 4], BF16, align_bytes=64)
+            grouped = work.tile([P, GROUP, P, 4], BF16, align_bytes=64, name="grouped")
             grouped_words = grouped[:].bitcast(F32)
             for h in range(GROUP // HALF):
-                xt = xt_pool.tile([P, HALF, 2, P], F32)
+                xt = xt_pool.tile([P, HALF, 2, P], F32, name="xt")
                 for a in range(HALF):
                     for u in range(2):
                         nc.tensor.transpose(
@@ -99,16 +108,22 @@ def tile_linear_pa_t_e_kernel(
                     out=grouped_words[:, h * HALF : (h + 1) * HALF, :, :],
                     in_=xt[:].rearrange("p a u r -> p a r u"),
                 )
-            x_codes = work.tile([P, GROUP * P], U32, align_bytes=64)
-            x_scales = work.tile([P, GROUP * P], U8, align_bytes=64)
+            grouped_of[i] = grouped
+
+        def quantise(i):
+            x_codes = work.tile([P, GROUP * P], U32, align_bytes=64, name="x_codes")
+            x_scales = work.tile([P, GROUP * P], U8, align_bytes=64, name="x_scales")
             nc.vector.quantize_mx(
                 out=x_codes[:].bitcast(FP8X4),
                 scales=x_scales[:],
-                in_=grouped[:].rearrange("p a r t -> p (a r t)"),
+                in_=grouped_of[i][:].rearrange("p a r t -> p (a r t)"),
             )
+            codes_of[i] = (x_codes, x_scales)
 
-            m1 = m_pool.tile([P, GROUP, RQ], F32)
-            m2 = m_pool.tile([P, GROUP, RQ], F32)
+        def multiply(i):
+            x_codes, x_scales = codes_of[i]
+            m1 = m_pool.tile([P, GROUP, RQ], F32, name="m1")
+            m2 = m_pool.tile([P, GROUP, RQ], F32, name="m2")
             for c, m in enumerate((m1, m2)):
                 for a in range(GROUP):
                     nc.tensor.matmul_mx(
@@ -120,35 +135,64 @@ def tile_linear_pa_t_e_kernel(
                         start=True,
                         stop=True,
                     )
+            m_of[i] = (m1, m2)
 
-            slots = slice(i * GROUP, (i + 1) * GROUP)
-            p1 = work.tile([P, GROUP, Q, R], F32)
+        def product1(i):
+            p1 = work.tile([P, GROUP, Q, R], F32, name="p1")
             nc.vector.tensor_tensor(
                 out=p1[:],
-                in0=m1[:].rearrange("p a (r q) -> p a q r", r=R),
-                in1=w0_sb[:, slots, :].unsqueeze(2).to_broadcast([P, GROUP, Q, R]),
+                in0=m_of[i][0][:].rearrange("p a (r q) -> p a q r", r=R),
+                in1=w0_sb[:, i * GROUP : (i + 1) * GROUP, :].unsqueeze(2).to_broadcast([P, GROUP, Q, R]),
                 op=MULT,
             )
-            w1 = work.tile([P, GROUP, Q], F32)
-            nc.vector.tensor_reduce(out=w1[:], in_=p1[:], axis=AXIS_X, op=ADD)
-            p2 = work.tile([P, GROUP, R, Q], F32)
+            p1_of[i] = p1
+
+        def sum1(i):
+            w1 = work.tile([P, GROUP, Q], F32, name="w1")
+            nc.vector.tensor_reduce(out=w1[:], in_=p1_of[i][:], axis=AXIS_X, op=ADD)
+            w1_of[i] = w1
+
+        def product2(i):
+            p2 = work.tile([P, GROUP, R, Q], F32, name="p2")
             nc.vector.tensor_tensor(
                 out=p2[:],
-                in0=m2[:].rearrange("p a (q r) -> p a r q", q=Q),
-                in1=w1[:].unsqueeze(2).to_broadcast([P, GROUP, R, Q]),
+                in0=m_of[i][1][:].rearrange("p a (q r) -> p a r q", q=Q),
+                in1=w1_of[i][:].unsqueeze(2).to_broadcast([P, GROUP, R, Q]),
                 op=MULT,
             )
-            part = i % STORE_ROUNDS
+            p2_of[i] = p2
+
+        def sum2(i):
+            batch, part = divmod(i, STORE_ROUNDS)
             if part == 0:
-                out_tile = work.tile([P, STORE_ROUNDS * GROUP, R], F32, name="out_tile")
+                out_of[batch] = out_pool.tile([P, STORE_ROUNDS * GROUP, R], F32, name="out_tile")
+            out_tile = out_of[batch]
             nc.vector.tensor_reduce(
                 out=out_tile[:, part * GROUP : (part + 1) * GROUP, :],
-                in_=p2[:],
+                in_=p2_of[i][:],
                 axis=AXIS_X,
                 op=ADD,
             )
             if part == STORE_ROUNDS - 1:
-                first = (i + 1 - STORE_ROUNDS) * GROUP
+                width = STORE_ROUNDS * GROUP
                 nc.sync.dma_start(
-                    out=out_view[:, first : first + STORE_ROUNDS * GROUP, :], in_=out_tile[:]
+                    out=out_view[:, batch * width : (batch + 1) * width, :], in_=out_tile[:]
                 )
+
+        def in_range(i):
+            return 0 <= i < ROUNDS
+
+        for s in range(ROUNDS + 3):
+            if in_range(s):
+                transpose(s)
+            if in_range(s - 2):
+                product1(s - 2)
+            if in_range(s - 1):
+                quantise(s - 1)
+                multiply(s - 1)
+            if in_range(s - 2):
+                sum1(s - 2)
+            if in_range(s - 3):
+                sum2(s - 3)
+            if in_range(s - 2):
+                product2(s - 2)

@@ -23,6 +23,7 @@ SLOTS = TOKENS // P
 GROUP = 4
 ROUNDS = SLOTS // GROUP
 HALF = 2
+PAIR = 2
 STORE_ROUNDS = 4
 
 FLOPS = 2 * TOKENS * D * 2 * RQ + 2 * TOKENS * 2 * RQ
@@ -153,27 +154,39 @@ def tile_linear_pa_t_e_kernel(
             w1_of[i] = w1
 
         def product2(i):
-            p2 = work.tile([P, GROUP, R, Q], F32, name="p2")
+            pair, part = divmod(i, PAIR)
+            if part == 0:
+                p2_of[pair] = work.tile([P, PAIR * GROUP, Q, R], F32, name="p2")
             nc.vector.tensor_tensor(
-                out=p2[:],
-                in0=m_of[i][1][:].rearrange("p a (q r) -> p a r q", q=Q),
-                in1=w1_of[i][:].unsqueeze(2).to_broadcast([P, GROUP, R, Q]),
+                out=p2_of[pair][:, part * GROUP : (part + 1) * GROUP, :, :],
+                in0=m_of[i][1][:].rearrange("p a (q r) -> p a q r", q=Q),
+                in1=w1_of[i][:].unsqueeze(3).to_broadcast([P, GROUP, Q, R]),
                 op=MULT,
             )
-            p2_of[i] = p2
 
-        def sum2(i):
-            batch, part = divmod(i, STORE_ROUNDS)
+        def sum2(pair):
+            pairs_in_store = STORE_ROUNDS // PAIR
+            batch, part = divmod(pair, pairs_in_store)
             if part == 0:
                 out_of[batch] = out_pool.tile([P, STORE_ROUNDS * GROUP, R], F32, name="out_tile")
             out_tile = out_of[batch]
-            nc.vector.tensor_reduce(
-                out=out_tile[:, part * GROUP : (part + 1) * GROUP, :],
-                in_=p2_of[i][:],
-                axis=AXIS_X,
+            blocks = PAIR * GROUP
+            terms = p2_of[pair]
+            half = Q // 2
+            while half > 1:
+                halved = work.tile([P, blocks, half, R], F32, name="halved%d" % half)
+                nc.gpsimd.tensor_tensor(
+                    out=halved[:], in0=terms[:, :, 0:half, :], in1=terms[:, :, half : 2 * half, :], op=ADD
+                )
+                terms = halved
+                half = half // 2
+            nc.gpsimd.tensor_tensor(
+                out=out_tile[:, part * blocks : (part + 1) * blocks, :],
+                in0=terms[:, :, 0, :],
+                in1=terms[:, :, 1, :],
                 op=ADD,
             )
-            if part == STORE_ROUNDS - 1:
+            if part == pairs_in_store - 1:
                 width = STORE_ROUNDS * GROUP
                 nc.sync.dma_start(
                     out=out_view[:, batch * width : (batch + 1) * width, :], in_=out_tile[:]
@@ -193,6 +206,6 @@ def tile_linear_pa_t_e_kernel(
             if in_range(s - 2):
                 sum1(s - 2)
             if in_range(s - 3):
-                sum2(s - 3)
-            if in_range(s - 2):
-                product2(s - 2)
+                product2(s - 3)
+                if (s - 3) % PAIR == PAIR - 1:
+                    sum2((s - 3) // PAIR)

@@ -23,7 +23,6 @@ SLOTS = TOKENS // P
 GROUP = 4
 ROUNDS = SLOTS // GROUP
 HALF = 2
-PAIR = 2
 STORE_ROUNDS = 4
 
 FLOPS = 2 * TOKENS * D * 2 * RQ + 2 * TOKENS * 2 * RQ
@@ -91,6 +90,7 @@ def tile_linear_pa_t_e_kernel(
         m_of = {}
         p1_of = {}
         w1_of = {}
+        m2_of = {}
         p2_of = {}
         out_of = {}
 
@@ -153,40 +153,33 @@ def tile_linear_pa_t_e_kernel(
             nc.vector.tensor_reduce(out=w1[:], in_=p1_of[i][:], axis=AXIS_X, op=ADD)
             w1_of[i] = w1
 
+        def copy_m2(i):
+            m2_sb = work.tile([P, GROUP, R, Q], F32, name="m2_sb")
+            nc.scalar.copy(out=m2_sb[:], in_=m_of[i][1][:].rearrange("p a (q r) -> p a r q", q=Q))
+            m2_of[i] = m2_sb
+
         def product2(i):
-            pair, part = divmod(i, PAIR)
-            if part == 0:
-                p2_of[pair] = work.tile([P, PAIR * GROUP, Q, R], F32, name="p2")
-            nc.vector.tensor_tensor(
-                out=p2_of[pair][:, part * GROUP : (part + 1) * GROUP, :, :],
-                in0=m_of[i][1][:].rearrange("p a (q r) -> p a q r", q=Q),
-                in1=w1_of[i][:].unsqueeze(3).to_broadcast([P, GROUP, Q, R]),
+            p2 = work.tile([P, GROUP, R, Q], F32, name="p2")
+            nc.gpsimd.tensor_tensor(
+                out=p2[:],
+                in0=m2_of[i][:],
+                in1=w1_of[i][:].unsqueeze(2).to_broadcast([P, GROUP, R, Q]),
                 op=MULT,
             )
+            p2_of[i] = p2
 
-        def sum2(pair):
-            pairs_in_store = STORE_ROUNDS // PAIR
-            batch, part = divmod(pair, pairs_in_store)
+        def sum2(i):
+            batch, part = divmod(i, STORE_ROUNDS)
             if part == 0:
                 out_of[batch] = out_pool.tile([P, STORE_ROUNDS * GROUP, R], F32, name="out_tile")
             out_tile = out_of[batch]
-            blocks = PAIR * GROUP
-            terms = p2_of[pair]
-            half = Q // 2
-            while half > 1:
-                halved = work.tile([P, blocks, half, R], F32, name="halved%d" % half)
-                nc.gpsimd.tensor_tensor(
-                    out=halved[:], in0=terms[:, :, 0:half, :], in1=terms[:, :, half : 2 * half, :], op=ADD
-                )
-                terms = halved
-                half = half // 2
-            nc.gpsimd.tensor_tensor(
-                out=out_tile[:, part * blocks : (part + 1) * blocks, :],
-                in0=terms[:, :, 0, :],
-                in1=terms[:, :, 1, :],
+            nc.vector.tensor_reduce(
+                out=out_tile[:, part * GROUP : (part + 1) * GROUP, :],
+                in_=p2_of[i][:],
+                axis=AXIS_X,
                 op=ADD,
             )
-            if part == pairs_in_store - 1:
+            if part == STORE_ROUNDS - 1:
                 width = STORE_ROUNDS * GROUP
                 nc.sync.dma_start(
                     out=out_view[:, batch * width : (batch + 1) * width, :], in_=out_tile[:]
@@ -195,17 +188,18 @@ def tile_linear_pa_t_e_kernel(
         def in_range(i):
             return 0 <= i < ROUNDS
 
-        for s in range(ROUNDS + 3):
+        for s in range(ROUNDS + 4):
+            if in_range(s - 2):
+                copy_m2(s - 2)
             if in_range(s):
                 transpose(s)
-            if in_range(s - 2):
-                product1(s - 2)
+            if in_range(s - 3):
+                sum1(s - 3)
+                product2(s - 3)
             if in_range(s - 1):
                 quantise(s - 1)
                 multiply(s - 1)
             if in_range(s - 2):
-                sum1(s - 2)
-            if in_range(s - 3):
-                product2(s - 3)
-                if (s - 3) % PAIR == PAIR - 1:
-                    sum2((s - 3) // PAIR)
+                product1(s - 2)
+            if in_range(s - 4):
+                sum2(s - 4)

@@ -154,16 +154,16 @@ def tile_linear_pa_t_e_kernel(
             w1_of[i] = w1
 
         def copy_m2(i):
-            m2_sb = work.tile([P, GROUP, R, Q], F32, name="m2_sb")
-            nc.scalar.copy(out=m2_sb[:], in_=m_of[i][1][:].rearrange("p a (q r) -> p a r q", q=Q))
+            m2_sb = work.tile([P, GROUP, Q, R], F32, name="m2_sb")
+            nc.scalar.copy(out=m2_sb[:], in_=m_of[i][1][:].rearrange("p a (q r) -> p a q r", q=Q))
             m2_of[i] = m2_sb
 
         def product2(i):
-            p2 = work.tile([P, GROUP, R, Q], F32, name="p2")
+            p2 = work.tile([P, GROUP, Q, R], F32, name="p2")
             nc.gpsimd.tensor_tensor(
                 out=p2[:],
                 in0=m2_of[i][:],
-                in1=w1_of[i][:].unsqueeze(2).to_broadcast([P, GROUP, R, Q]),
+                in1=w1_of[i][:].unsqueeze(3).to_broadcast([P, GROUP, Q, R]),
                 op=MULT,
             )
             p2_of[i] = p2
@@ -175,7 +175,7 @@ def tile_linear_pa_t_e_kernel(
             out_tile = out_of[batch]
             nc.vector.tensor_reduce(
                 out=out_tile[:, part * GROUP : (part + 1) * GROUP, :],
-                in_=p2_of[i][:],
+                in_=p2_of[i][:].rearrange("p a q r -> p a r q"),
                 axis=AXIS_X,
                 op=ADD,
             )

from contextlib import ExitStack

import concourse.mybir as mybir
from concourse.masks import make_identity

F32 = mybir.dt.float32
BF16 = mybir.dt.bfloat16
I32 = mybir.dt.int32
U32 = mybir.dt.uint32
U8 = mybir.dt.uint8
FP8X4 = mybir.dt.float8_e4m3fn_x4
MULT = mybir.AluOpType.mult
ADD = mybir.AluOpType.add
AXIS_X = mybir.AxisListType.X

P = 128
D = 512
R = 8
Q = 16
RQ = R * Q
TOKENS = 4 * 4096
SLOTS = TOKENS // P
GROUP = 4
ROUNDS = SLOTS // GROUP
HALF = 2
STORE_ROUNDS = 4

FLOPS = 2 * TOKENS * D * 2 * RQ + 2 * TOKENS * 2 * RQ


def tile_linear_pa_t_e_kernel(
    tc, x, w0, core1_words, core1_scales, core2_words, core2_scales, out
):
    nc = tc.nc
    x_view = x.flatten_outer_dims().rearrange("(p j) d -> p j d", j=SLOTS)
    w0_view = w0.flatten_outer_dims().rearrange("(p j) r -> p j r", j=SLOTS)
    out_view = out.flatten_outer_dims().rearrange("(p j) r -> p j r", j=SLOTS)

    with ExitStack() as stack:
        keep = stack.enter_context(tc.tile_pool(name="keep", bufs=1))
        x_pool = stack.enter_context(tc.tile_pool(name="x_pool", bufs=ROUNDS))
        out_pool = stack.enter_context(tc.tile_pool(name="out_pool", bufs=ROUNDS // STORE_ROUNDS))
        work = stack.enter_context(tc.tile_pool(name="work", bufs=3))
        xt_pool = stack.enter_context(tc.psum_pool(name="xt_pool", bufs=4))
        m_pool = stack.enter_context(tc.psum_pool(name="m_pool", bufs=2))
        stack.enter_context(tc.manual_schedule())

        core_scales = keep.tile([P, 2 * RQ], U8, align_bytes=64)
        nc.vector.memset(core_scales[:].bitcast(I32), 0)
        identity = keep.tile([P, P], F32)
        make_identity(nc, identity[:])

        x_tiles = []

        def load_x(i):
            x_tile = x_pool.tile([P, GROUP, D], BF16, name="x_tile")
            nc.sync.dma_start(out=x_tile[:], in_=x_view[:, i * GROUP : (i + 1) * GROUP, :])
            x_tiles.append(x_tile)

        load_x(0)

        core_codes = keep.tile([P, 2 * RQ], U32, align_bytes=64)
        nc.sync.dma_start(
            out=core_codes[:, 0:RQ].bitcast(I32).rearrange("p (g n) -> p g n", g=R),
            in_=core1_words.rearrange("g p n t -> p g (n t)").bitcast(I32),
        )
        nc.sync.dma_start(
            out=core_codes[:, RQ : 2 * RQ].bitcast(I32).rearrange("p (g n) -> p g n", g=Q),
            in_=core2_words.rearrange("g p n t -> p g (n t)").bitcast(I32),
        )
        for quadrant in range(4):
            rows = slice(32 * quadrant, 32 * quadrant + 4)
            blocks = slice(4 * quadrant, 4 * quadrant + 4)
            nc.sync.dma_start(
                out=core_scales[rows, 0:RQ].bitcast(I32).rearrange("j (g n) -> j g n", g=R),
                in_=core1_scales[:, blocks, :].rearrange("g j n -> j g n").bitcast(I32),
            )
            nc.sync.dma_start(
                out=core_scales[rows, RQ : 2 * RQ].bitcast(I32).rearrange("j (g n) -> j g n", g=Q),
                in_=core2_scales[:, blocks, :].rearrange("g j n -> j g n").bitcast(I32),
            )
        w0_sb = keep.tile([P, SLOTS, R], BF16)
        nc.sync.dma_start(out=w0_sb[:], in_=w0_view)

        for i in range(1, ROUNDS):
            load_x(i)

        grouped_of = {}
        codes_of = {}
        m_of = {}
        p1_of = {}
        w1_of = {}
        m2_of = {}
        p2_of = {}
        out_of = {}

        def transpose(i):
            x_words = x_tiles[i][:].bitcast(F32)
            grouped = work.tile([P, GROUP, P, 4], BF16, align_bytes=64, name="grouped")
            grouped_words = grouped[:].bitcast(F32)
            for h in range(GROUP // HALF):
                xt = xt_pool.tile([P, HALF, 2, P], F32, name="xt")
                for a in range(HALF):
                    for u in range(2):
                        nc.tensor.transpose(
                            xt[:, a, u, :], x_words[:, h * HALF + a, u : D // 2 : 2], identity[:]
                        )
                nc.scalar.copy(
                    out=grouped_words[:, h * HALF : (h + 1) * HALF, :, :],
                    in_=xt[:].rearrange("p a u r -> p a r u"),
                )
            grouped_of[i] = grouped

        def quantise(i):
            x_codes = work.tile([P, GROUP * P], U32, align_bytes=64, name="x_codes")
            x_scales = work.tile([P, GROUP * P], U8, align_bytes=64, name="x_scales")
            nc.vector.quantize_mx(
                out=x_codes[:].bitcast(FP8X4),
                scales=x_scales[:],
                in_=grouped_of[i][:].rearrange("p a r t -> p (a r t)"),
            )
            codes_of[i] = (x_codes, x_scales)

        def multiply(i):
            x_codes, x_scales = codes_of[i]
            m1 = m_pool.tile([P, GROUP, RQ], F32, name="m1")
            m2 = m_pool.tile([P, GROUP, RQ], F32, name="m2")
            for c, m in enumerate((m1, m2)):
                for a in range(GROUP):
                    nc.tensor.matmul_mx(
                        out=m[:, a, :],
                        lhsT=x_codes[:, a * P : (a + 1) * P].bitcast(FP8X4),
                        lhsT_scale=x_scales[:, a * P : (a + 1) * P],
                        rhs=core_codes[:, c * RQ : (c + 1) * RQ].bitcast(FP8X4),
                        rhs_scale=core_scales[:, c * RQ : (c + 1) * RQ],
                        start=True,
                        stop=True,
                    )
            m_of[i] = (m1, m2)

        def product1(i):
            p1 = work.tile([P, GROUP, Q, R], F32, name="p1")
            nc.vector.tensor_tensor(
                out=p1[:],
                in0=m_of[i][0][:].rearrange("p a (r q) -> p a q r", r=R),
                in1=w0_sb[:, i * GROUP : (i + 1) * GROUP, :].unsqueeze(2).to_broadcast([P, GROUP, Q, R]),
                op=MULT,
            )
            p1_of[i] = p1

        def sum1(i):
            w1 = work.tile([P, GROUP, Q], F32, name="w1")
            nc.vector.tensor_reduce(out=w1[:], in_=p1_of[i][:], axis=AXIS_X, op=ADD)
            w1_of[i] = w1

        def copy_m2(i):
            m2_sb = work.tile([P, GROUP, Q, R], F32, name="m2_sb")
            nc.scalar.copy(out=m2_sb[:], in_=m_of[i][1][:].rearrange("p a (q r) -> p a q r", q=Q))
            m2_of[i] = m2_sb

        def product2(i):
            p2 = work.tile([P, GROUP, Q, R], F32, name="p2")
            nc.gpsimd.tensor_tensor(
                out=p2[:],
                in0=m2_of[i][:],
                in1=w1_of[i][:].unsqueeze(3).to_broadcast([P, GROUP, Q, R]),
                op=MULT,
            )
            p2_of[i] = p2

        def sum2(i):
            batch, part = divmod(i, STORE_ROUNDS)
            if part == 0:
                out_of[batch] = out_pool.tile([P, STORE_ROUNDS * GROUP, R], F32, name="out_tile")
            out_tile = out_of[batch]
            nc.vector.tensor_reduce(
                out=out_tile[:, part * GROUP : (part + 1) * GROUP, :],
                in_=p2_of[i][:].rearrange("p a q r -> p a r q"),
                axis=AXIS_X,
                op=ADD,
            )
            if part == STORE_ROUNDS - 1:
                width = STORE_ROUNDS * GROUP
                nc.sync.dma_start(
                    out=out_view[:, batch * width : (batch + 1) * width, :], in_=out_tile[:]
                )

        def in_range(i):
            return 0 <= i < ROUNDS

        for s in range(ROUNDS + 4):
            if in_range(s - 2):
                copy_m2(s - 2)
            if in_range(s):
                transpose(s)
            if in_range(s - 3):
                sum1(s - 3)
                product2(s - 3)
            if in_range(s - 1):
                quantise(s - 1)
                multiply(s - 1)
            if in_range(s - 2):
                product1(s - 2)
            if in_range(s - 4):
                sum2(s - 4)
